import numpy as np
import ml_dtypes


def mxq(x, axis, fmt="e4m3"):
    dtype, down = {"e4m3": (ml_dtypes.float8_e4m3fn, 7), "e5m2": (ml_dtypes.float8_e5m2, 14)}[fmt]
    v = np.moveaxis(np.asarray(x, np.float32).astype(ml_dtypes.bfloat16).astype(np.float64), axis, -1)
    blocks = v.reshape(v.shape[:-1] + (-1, 32))
    amax = np.abs(blocks).max(-1, keepdims=True)
    byte = np.maximum(np.where(amax > 0, np.frexp(amax)[1] - 1 + 127, 0) - down, 1)
    scale = np.exp2(byte - 127.0)
    codes = (blocks / scale).astype(np.float32).astype(dtype).astype(np.float64)
    return np.moveaxis((codes * scale).reshape(v.shape), -1, axis)


WIDE = False


def mx_kscale(k):
    if not WIDE:
        return np.ones(k)
    levels = np.array([10, -10, 5, -5, 0])
    if k % 512:
        return np.exp2(np.random.permutation(np.resize(levels, k // 32))).repeat(32)
    a = np.empty((k // 512, 16))
    for p in range(k // 512):
        a[p, :8] = np.random.permutation(np.resize(levels, 8))
        for g in range(8):
            far = levels[np.abs(levels - a[p, g]) >= 10]
            a[p, g + 8] = far[np.random.randint(len(far))]
    return np.exp2(a.ravel()).repeat(32)


BF16 = ml_dtypes.bfloat16


def bf(x):
    return np.asarray(x, np.float32).astype(BF16)


def f64(x):
    return np.asarray(x).astype(np.float64)


B, C, HH, WW = 1, 512, 32, 32
N = HH * WW


def setup_inputs():
    s, t = mx_kscale(C), mx_kscale(C)
    return {"x": bf(np.random.standard_normal((B, C, HH, WW)) * s[None, :, None, None]),
            "Wq": bf(np.random.standard_normal((C, C)) * 1.4 / np.sqrt(C) * t[:, None] / s[None, :]),
            "bq": bf(np.random.standard_normal(C) * 0.2 * t),
            "k": bf(np.random.standard_normal((B, N, C)) * 1.4 / t)}


def reference(x, Wq, bq, k):
    xt = f64(x).reshape(B, C, N)
    q = f64(bf(mxq(xt, 1, "e4m3").transpose(0, 2, 1) @ mxq(f64(Wq), 1, "e4m3").T)) + f64(bq)
    scores = mxq(q / np.sqrt(C), 2, "e4m3") @ mxq(f64(k), 2, "e4m3").transpose(0, 2, 1)
    e = np.exp(scores - scores.max(-1, keepdims=True))
    return e / e.sum(-1, keepdims=True)

@@ -1,0 +1,304 @@
+from contextlib import ExitStack
+import math
+
+import concourse.mybir as mybir
+from concourse.masks import make_identity
+
+F32 = mybir.dt.float32
+BF16 = mybir.dt.bfloat16
+U32 = mybir.dt.uint32
+U8 = mybir.dt.uint8
+FP8X4 = mybir.dt.float8_e4m3fn_x4
+ALU = mybir.AluOpType
+ACT = mybir.ActivationFunctionType
+AX = mybir.AxisListType
+
+P = 128
+C = 512
+NTOK = 1024
+NT = NTOK // P
+QBANK = BF16
+
+FLOPS = 2 * NTOK * C * C + 2 * NTOK * NTOK * C
+
+X_CHUNKS = (256, 256, 512)
+AHEAD = 3
+V_TAIL = 3
+
+
+def tile_visionattention_pa_kernel(tc, x, Wq, bq, k, out):
+    nc = tc.nc
+    inv_sqrt_c = 1.0 / math.sqrt(C)
+
+    with ExitStack() as ctx:
+        const = ctx.enter_context(tc.tile_pool(name="const", bufs=1))
+        keep = ctx.enter_context(tc.tile_pool(name="keep", bufs=1))
+        soft = ctx.enter_context(tc.tile_pool(name="soft", bufs=5))
+        stat = ctx.enter_context(tc.tile_pool(name="stat", bufs=6))
+        psum = ctx.enter_context(tc.psum_pool(name="psum", bufs=8))
+        ctx.enter_context(tc.manual_schedule())
+
+        bq_raw = const.tile([P, 4], BF16, name="bq_raw")
+        nc.scalar.dma_start(out=bq_raw[:], in_=bq.rearrange("(p t) -> p t", t=4))
+
+        w_view = Wq.rearrange("(m t) c -> m t c", t=4)
+        x_view = x[0].rearrange("(p j) h w -> p j (h w)", j=4)
+        k_view = k[0].rearrange("(g r b) c -> r g b c", r=P, b=2)
+        w_raw = {}
+        x_raw = {}
+        k_raw = {}
+
+        def load_w(b):
+            w_raw[b] = keep.tile([P, 2, C], BF16, name="w_raw%d" % b)
+            nc.sync.dma_start(out=w_raw[b][:], in_=w_view[:, 2 * b : 2 * b + 2, :])
+
+        def load_x(c):
+            n0 = sum(X_CHUNKS[:c])
+            x_raw[c] = keep.tile([P, 4, X_CHUNKS[c]], BF16, name="x_raw%d" % c)
+            nc.sync.dma_start(out=x_raw[c][:], in_=x_view[:, :, n0 : n0 + X_CHUNKS[c]])
+
+        def load_k(g):
+            k_raw[g] = keep.tile([P, 2, C], BF16, name="k_raw%d" % g)
+            nc.sync.dma_start(out=k_raw[g][:], in_=k_view[:, g, :, :])
+
+        load_w(0)
+        load_w(1)
+        load_k(0)
+        load_x(0)
+        load_k(1)
+        load_k(2)
+        load_x(1)
+        load_k(3)
+        load_x(2)
+
+        ident = const.tile([P, P], F32, name="ident")
+        make_identity(nc, ident[:])
+        warm_in = const.tile([P, 1], F32, name="warm_in")
+        warm_out = const.tile([P, 1], F32, name="warm_out")
+        nc.vector.memset(warm_in[:], 0.0)
+        nc.scalar.activation(out=warm_out[:], in_=warm_in[:], func=ACT.Exp)
+        bias_s = const.tile([P, 4], F32, name="bias_s")
+
+        def turn(raw, name):
+            words = raw[:].rearrange("r s c -> r (s c)").bitcast(F32)
+            bank = psum.tile([P, 2, 2, P], F32, tag="bank", name=name)
+            for s in range(2):
+                for u in range(2):
+                    nc.tensor.transpose(bank[:, s, u, :], words[:, 256 * s + u : 256 * (s + 1) : 2], ident[:])
+            return bank
+
+        w_grp = keep.tile([P, 4 * C], BF16, name="w_grp", align_bytes=64)
+        w_codes = keep.tile([P, C], U32, name="w_codes", align_bytes=64)
+        w_scales = keep.tile([P, C], U8, name="w_scales", align_bytes=64)
+
+        def turn_w(b):
+            bank = turn(w_raw[b], "wt%d" % b)
+            nc.scalar.copy(
+                out=w_grp[:].bitcast(F32)[:, 512 * b : 512 * (b + 1)].rearrange("p (s r u) -> p s r u", s=2, u=2),
+                in_=bank[:].rearrange("p s u r -> p s r u"),
+            )
+
+        x_grp = {}
+        x_codes = {}
+        x_scales = {}
+
+        def group_x(c, engine):
+            x_grp[c] = keep.tile([P, X_CHUNKS[c], 4], BF16, name="x_grp%d" % c, align_bytes=64)
+            src = x_raw[c][:].rearrange("p j n -> p n j")
+            if engine == "scalar":
+                nc.scalar.copy(out=x_grp[c][:], in_=src)
+            else:
+                nc.vector.tensor_copy(out=x_grp[c][:], in_=src)
+
+        def quant_x(c):
+            x_codes[c] = keep.tile([P, X_CHUNKS[c]], U32, name="x_codes%d" % c, align_bytes=64)
+            x_scales[c] = keep.tile([P, X_CHUNKS[c]], U8, name="x_scales%d" % c, align_bytes=64)
+            nc.vector.quantize_mx(
+                out=x_codes[c][:].bitcast(FP8X4), scales=x_scales[c][:], in_=x_grp[c][:].rearrange("p n j -> p (n j)")
+            )
+
+        k_grp = {}
+        for h in range(2):
+            k_grp[h] = keep.tile([P, 4 * C], BF16, name="k_grp%d" % h, align_bytes=64)
+        k_codes = {}
+        k_scales = {}
+
+        def turn_k(g):
+            bank = turn(k_raw[g], "kt%d" % g)
+            nc.scalar.copy(
+                out=k_grp[g // 2][:].bitcast(F32)[:, 512 * (g % 2) : 512 * (g % 2 + 1)].rearrange("p (r q) -> p r q", q=4),
+                in_=bank[:].rearrange("p b u r -> p r (b u)"),
+            )
+
+        def quant_k(h):
+            k_codes[h] = keep.tile([P, C], U32, name="k_codes%d" % h, align_bytes=64)
+            k_scales[h] = keep.tile([P, C], U8, name="k_scales%d" % h, align_bytes=64)
+            nc.vector.quantize_mx(out=k_codes[h][:].bitcast(FP8X4), scales=k_scales[h][:], in_=k_grp[h][:])
+
+        chunk_of = []
+        for c in range(len(X_CHUNKS)):
+            for j in range(X_CHUNKS[c] // P):
+                chunk_of.append((c, j))
+
+        q_bank = {}
+        q_grp = {}
+        q_codes = {}
+        q_scales = {}
+
+        def project(i):
+            c, j = chunk_of[i]
+            if c not in x_codes:
+                quant_x(c)
+            q_bank[i] = psum.tile([P, 4, P], QBANK, tag="bank", name="qp")
+            for t in range(4):
+                nc.tensor.matmul_mx(
+                    out=q_bank[i][:, t, :],
+                    lhsT=w_codes[:, P * t : P * (t + 1)].bitcast(FP8X4),
+                    lhsT_scale=w_scales[:, P * t : P * (t + 1)],
+                    rhs=x_codes[c][:, P * j : P * (j + 1)].bitcast(FP8X4),
+                    rhs_scale=x_scales[c][:, P * j : P * (j + 1)],
+                    start=True,
+                    stop=True,
+                )
+
+        def read_q(i):
+            q_grp[i] = keep.tile([P, P, 4], BF16, name="q_grp%d" % i, align_bytes=64)
+            nc.vector.scalar_tensor_tensor(
+                out=q_grp[i][:],
+                in0=q_bank[i][:].rearrange("p t n -> p n t"),
+                scalar=inv_sqrt_c,
+                in1=bias_s[:].unsqueeze(1).to_broadcast([P, P, 4]),
+                op0=ALU.mult,
+                op1=ALU.add,
+            )
+
+        def quant_q(i):
+            q_codes[i] = keep.tile([P, P], U32, name="q_codes%d" % i, align_bytes=64)
+            q_scales[i] = keep.tile([P, P], U8, name="q_scales%d" % i, align_bytes=64)
+            nc.vector.quantize_mx(
+                out=q_codes[i][:].bitcast(FP8X4), scales=q_scales[i][:], in_=q_grp[i][:].rearrange("p n t -> p (n t)")
+            )
+
+        sc = {}
+        mx = {}
+        ex = {}
+        ssum = {}
+        tot = {}
+
+        def scores(i):
+            sc[i] = []
+            for h in range(2):
+                s_h = psum.tile([P, C], F32, tag="bank", name="sc%d" % h)
+                nc.tensor.matmul_mx(
+                    out=s_h[:],
+                    lhsT=q_codes[i][:].bitcast(FP8X4),
+                    lhsT_scale=q_scales[i][:],
+                    rhs=k_codes[h][:].bitcast(FP8X4),
+                    rhs_scale=k_scales[h][:],
+                    start=True,
+                    stop=True,
+                )
+                sc[i].append(s_h)
+
+        def bank_max(i, h):
+            if h == 0:
+                mx[i] = stat.tile([P, 2], F32, name="mx")
+            nc.vector.tensor_reduce(out=mx[i][:, h : h + 1], in_=sc[i][h][:], axis=AX.X, op=ALU.max)
+
+        def exponentials(i):
+            nm = stat.tile([P, 1], F32, name="nmax")
+            nc.vector.tensor_scalar(
+                out=nm[:], in0=mx[i][:, 0:1], scalar1=mx[i][:, 1:2], scalar2=-1.0, op0=ALU.max, op1=ALU.mult
+            )
+            ex[i] = soft.tile([P, NTOK], F32, name="e")
+            ssum[i] = stat.tile([P, 2], F32, name="ssum")
+            for h in range(2):
+                nc.scalar.activation(
+                    out=ex[i][:, C * h : C * (h + 1)],
+                    in_=sc[i][h][:],
+                    func=ACT.Exp,
+                    bias=nm[:],
+                    scale=1.0,
+                    accum_out=ssum[i][:, h : h + 1],
+                )
+
+        def row_sum(i):
+            tot[i] = stat.tile([P, 1], F32, name="tot")
+            nc.vector.tensor_reduce(out=tot[i][:], in_=ssum[i][:], axis=AX.X, op=ALU.add)
+
+        def finish(i):
+            rinv = stat.tile([P, 1], F32, name="rinv")
+            nc.vector.reciprocal(out=rinv[:], in_=tot[i][:])
+            o = soft.tile([P, NTOK], F32, name="o")
+            for h in range(2):
+                cols = slice(C * h, C * (h + 1))
+                if i >= NT - V_TAIL:
+                    nc.vector.tensor_scalar(out=o[:, cols], in0=ex[i][:, cols], scalar1=rinv[:], scalar2=None, op0=ALU.mult)
+                else:
+                    nc.gpsimd.tensor_scalar(
+                        out=o[:, cols], in0=ex[i][:, cols], scalar1=rinv[:], scalar2=0.0, op0=ALU.mult, op1=ALU.add
+                    )
+                nc.sync.dma_start(out=out[0, P * i : P * (i + 1), cols], in_=o[:, cols])
+
+        turn_w(0)
+        turn_w(1)
+        group_x(0, "vector")
+        nc.vector.quantize_mx(out=w_codes[:].bitcast(FP8X4), scales=w_scales[:], in_=w_grp[:])
+        quant_x(0)
+        nc.vector.tensor_scalar(out=bias_s[:], in0=bq_raw[:], scalar1=inv_sqrt_c, scalar2=None, op0=ALU.mult)
+        turn_k(0)
+        turn_k(1)
+        turn_k(2)
+        group_x(1, "scalar")
+        project(0)
+        quant_k(0)
+        project(1)
+        read_q(0)
+        read_q(1)
+        quant_q(0)
+        quant_x(1)
+        turn_k(3)
+        quant_q(1)
+        project(2)
+        group_x(2, "scalar")
+        quant_k(1)
+        scores(0)
+        scores(1)
+        read_q(2)
+
+        big = []
+        for i in range(NT):
+            big.append(("max", i, 0))
+            big.append(("max", i, 1))
+            if i + AHEAD < NT:
+                big.append(("read_q", i + AHEAD, 0))
+        pending = [(1, 1, AHEAD - 1)]
+        done = 0
+        while done < len(big) or pending:
+            if done < len(big):
+                kind, i, h = big[done]
+                if kind == "max":
+                    if h == 0 and i + AHEAD < NT:
+                        project(i + AHEAD)
+                    bank_max(i, h)
+                    if h == 1:
+                        pending.append((done + 2, 0, i))
+                else:
+                    read_q(i)
+                    pending.append((done + 2, 1, i))
+            done += 1
+            ready = sorted(p for p in pending if p[0] <= done)
+            ready = sorted(ready, key=lambda p: (p[1], p[2]))
+            pending = [p for p in pending if p[0] > done]
+            for due, rank, i in ready:
+                if rank == 0:
+                    exponentials(i)
+                    pending.append((done + 3, 2, i))
+                elif rank == 1:
+                    quant_q(i)
+                    scores(i)
+                elif rank == 2:
+                    row_sum(i)
+                    pending.append((done + 1, 3, i))
+                else:
+                    finish(i)

@@ -207,9 +207,7 @@ def tile_visionattention_pa_kernel(tc, x, Wq, bq, k, out):
 
         def exponentials(i):
             nm = stat.tile([P, 1], F32, name="nmax")
-            nc.vector.tensor_scalar(
-                out=nm[:], in0=mx[i][:, 0:1], scalar1=mx[i][:, 1:2], scalar2=-1.0, op0=ALU.max, op1=ALU.mult
-            )
+            nc.vector.tensor_reduce(out=nm[:], in_=mx[i][:], axis=AX.X, op=ALU.max, negate=True)
             ex[i] = soft.tile([P, NTOK], F32, name="e")
             ssum[i] = stat.tile([P, 2], F32, name="ssum")
             for h in range(2):

@@ -17,13 +17,30 @@ P = 128
 C = 512
 NTOK = 1024
 NT = NTOK // P
-QBANK = BF16
 
 FLOPS = 2 * NTOK * C * C + 2 * NTOK * NTOK * C
 
 X_CHUNKS = (256, 256, 512)
-AHEAD = 3
-V_TAIL = 3
+LOADS = ("w0", "w1", "x0", "k0", "k1", "x1", "k2", "k3", "x2")
+SC_BUFS = 6
+QP_BUFS = 2
+GX = ("vector", "scalar", "scalar")
+CW = ("scalar", "scalar")
+CK = ("scalar", "vector", "scalar", "scalar")
+NORM = (("g", "g"), ("g", "g"), ("g", "g"), ("g", "g"), ("g", "g"), ("g", "g"), ("v", "v"), ("v", "v"))
+RS = ()
+HEAD_TILES = 3
+PE_HEAD = (
+    ("tw", 0, 0), ("tw", 1, 0), ("tk", 0, 0), ("tk", 1, 0), ("P", 0, 0), ("P", 1, 0),
+    ("tk", 2, 0), ("tk", 3, 0), ("SC", 0, 0), ("P", 2, 0), ("SC", 0, 1), ("SC", 1, 0), ("SC", 1, 1),
+)
+V_HEAD = (
+    ("gx", 0, 0), ("qw", 0, 0), ("qx", 0, 0), ("bias", 0, 0), ("ck", 1, 0), ("R", 0, 0), ("R", 1, 0), ("qk", 0, 0), ("Q", 0, 0),
+    ("qx", 1, 0), ("Q", 1, 0), ("qk", 1, 0), ("R", 2, 0),
+)
+S_HEAD = (
+    ("cw", 0, 0), ("cw", 1, 0), ("ck", 0, 0), ("gx", 1, 0), ("ck", 2, 0), ("ck", 3, 0), ("gx", 2, 0),
+)
 
 
 def tile_visionattention_pa_kernel(tc, x, Wq, bq, k, out):
@@ -33,9 +50,8 @@ def tile_visionattention_pa_kernel(tc, x, Wq, bq, k, out):
     with ExitStack() as ctx:
         const = ctx.enter_context(tc.tile_pool(name="const", bufs=1))
         keep = ctx.enter_context(tc.tile_pool(name="keep", bufs=1))
-        soft = ctx.enter_context(tc.tile_pool(name="soft", bufs=5))
-        stat = ctx.enter_context(tc.tile_pool(name="stat", bufs=6))
-        psum = ctx.enter_context(tc.psum_pool(name="psum", bufs=8))
+        scp = ctx.enter_context(tc.psum_pool(name="scp", bufs=SC_BUFS))
+        qpp = ctx.enter_context(tc.psum_pool(name="qpp", bufs=QP_BUFS))
         ctx.enter_context(tc.manual_schedule())
 
         bq_raw = const.tile([P, 4], BF16, name="bq_raw")
@@ -47,29 +63,18 @@ def tile_visionattention_pa_kernel(tc, x, Wq, bq, k, out):
         w_raw = {}
         x_raw = {}
         k_raw = {}
-
-        def load_w(b):
-            w_raw[b] = keep.tile([P, 2, C], BF16, name="w_raw%d" % b)
-            nc.sync.dma_start(out=w_raw[b][:], in_=w_view[:, 2 * b : 2 * b + 2, :])
-
-        def load_x(c):
-            n0 = sum(X_CHUNKS[:c])
-            x_raw[c] = keep.tile([P, 4, X_CHUNKS[c]], BF16, name="x_raw%d" % c)
-            nc.sync.dma_start(out=x_raw[c][:], in_=x_view[:, :, n0 : n0 + X_CHUNKS[c]])
-
-        def load_k(g):
-            k_raw[g] = keep.tile([P, 2, C], BF16, name="k_raw%d" % g)
-            nc.sync.dma_start(out=k_raw[g][:], in_=k_view[:, g, :, :])
-
-        load_w(0)
-        load_w(1)
-        load_k(0)
-        load_x(0)
-        load_k(1)
-        load_k(2)
-        load_x(1)
-        load_k(3)
-        load_x(2)
+        for name in LOADS:
+            n = int(name[1:])
+            if name[0] == "w":
+                w_raw[n] = keep.tile([P, 2, C], BF16, name="w_raw%d" % n)
+                nc.sync.dma_start(out=w_raw[n][:], in_=w_view[:, 2 * n : 2 * n + 2, :])
+            elif name[0] == "x":
+                n0 = sum(X_CHUNKS[:n])
+                x_raw[n] = keep.tile([P, 4, X_CHUNKS[n]], BF16, name="x_raw%d" % n)
+                nc.sync.dma_start(out=x_raw[n][:], in_=x_view[:, :, n0 : n0 + X_CHUNKS[n]])
+            else:
+                k_raw[n] = keep.tile([P, 2, C], BF16, name="k_raw%d" % n)
+                nc.sync.dma_start(out=k_raw[n][:], in_=k_view[:, n, :, :])
 
         ident = const.tile([P, P], F32, name="ident")
         make_identity(nc, ident[:])
@@ -79,224 +84,287 @@ def tile_visionattention_pa_kernel(tc, x, Wq, bq, k, out):
         nc.scalar.activation(out=warm_out[:], in_=warm_in[:], func=ACT.Exp)
         bias_s = const.tile([P, 4], F32, name="bias_s")
 
-        def turn(raw, name):
-            words = raw[:].rearrange("r s c -> r (s c)").bitcast(F32)
-            bank = psum.tile([P, 2, 2, P], F32, tag="bank", name=name)
-            for s in range(2):
-                for u in range(2):
-                    nc.tensor.transpose(bank[:, s, u, :], words[:, 256 * s + u : 256 * (s + 1) : 2], ident[:])
-            return bank
-
         w_grp = keep.tile([P, 4 * C], BF16, name="w_grp", align_bytes=64)
         w_codes = keep.tile([P, C], U32, name="w_codes", align_bytes=64)
         w_scales = keep.tile([P, C], U8, name="w_scales", align_bytes=64)
-
-        def turn_w(b):
-            bank = turn(w_raw[b], "wt%d" % b)
-            nc.scalar.copy(
-                out=w_grp[:].bitcast(F32)[:, 512 * b : 512 * (b + 1)].rearrange("p (s r u) -> p s r u", s=2, u=2),
-                in_=bank[:].rearrange("p s u r -> p s r u"),
-            )
-
-        x_grp = {}
-        x_codes = {}
-        x_scales = {}
-
-        def group_x(c, engine):
-            x_grp[c] = keep.tile([P, X_CHUNKS[c], 4], BF16, name="x_grp%d" % c, align_bytes=64)
-            src = x_raw[c][:].rearrange("p j n -> p n j")
-            if engine == "scalar":
-                nc.scalar.copy(out=x_grp[c][:], in_=src)
-            else:
-                nc.vector.tensor_copy(out=x_grp[c][:], in_=src)
-
-        def quant_x(c):
-            x_codes[c] = keep.tile([P, X_CHUNKS[c]], U32, name="x_codes%d" % c, align_bytes=64)
-            x_scales[c] = keep.tile([P, X_CHUNKS[c]], U8, name="x_scales%d" % c, align_bytes=64)
-            nc.vector.quantize_mx(
-                out=x_codes[c][:].bitcast(FP8X4), scales=x_scales[c][:], in_=x_grp[c][:].rearrange("p n j -> p (n j)")
-            )
-
         k_grp = {}
         for h in range(2):
             k_grp[h] = keep.tile([P, 4 * C], BF16, name="k_grp%d" % h, align_bytes=64)
-        k_codes = {}
-        k_scales = {}
 
-        def turn_k(g):
-            bank = turn(k_raw[g], "kt%d" % g)
-            nc.scalar.copy(
-                out=k_grp[g // 2][:].bitcast(F32)[:, 512 * (g % 2) : 512 * (g % 2 + 1)].rearrange("p (r q) -> p r q", q=4),
-                in_=bank[:].rearrange("p b u r -> p r (b u)"),
-            )
-
-        def quant_k(h):
-            k_codes[h] = keep.tile([P, C], U32, name="k_codes%d" % h, align_bytes=64)
-            k_scales[h] = keep.tile([P, C], U8, name="k_scales%d" % h, align_bytes=64)
-            nc.vector.quantize_mx(out=k_codes[h][:].bitcast(FP8X4), scales=k_scales[h][:], in_=k_grp[h][:])
+        T = {}
 
         chunk_of = []
         for c in range(len(X_CHUNKS)):
             for j in range(X_CHUNKS[c] // P):
                 chunk_of.append((c, j))
 
-        q_bank = {}
-        q_grp = {}
-        q_codes = {}
-        q_scales = {}
+        def copy_on(engine, dst, src):
+            if engine == "scalar":
+                nc.scalar.copy(out=dst, in_=src)
+            elif engine == "vector":
+                nc.vector.tensor_copy(out=dst, in_=src)
+            else:
+                nc.gpsimd.tensor_scalar(out=dst, in0=src, scalar1=1.0, scalar2=0.0, op0=ALU.mult, op1=ALU.add)
 
-        def project(i):
-            c, j = chunk_of[i]
-            if c not in x_codes:
-                quant_x(c)
-            q_bank[i] = psum.tile([P, 4, P], QBANK, tag="bank", name="qp")
-            for t in range(4):
-                nc.tensor.matmul_mx(
-                    out=q_bank[i][:, t, :],
-                    lhsT=w_codes[:, P * t : P * (t + 1)].bitcast(FP8X4),
-                    lhsT_scale=w_scales[:, P * t : P * (t + 1)],
-                    rhs=x_codes[c][:, P * j : P * (j + 1)].bitcast(FP8X4),
-                    rhs_scale=x_scales[c][:, P * j : P * (j + 1)],
-                    start=True,
-                    stop=True,
+        def turn(raw, name):
+            words = raw[:].rearrange("r s c -> r (s c)").bitcast(F32)
+            bank = scp.tile([P, 2, 2, P], F32, tag="sc", name=name)
+            for s in range(2):
+                for u in range(2):
+                    nc.tensor.transpose(bank[:, s, u, :], words[:, 256 * s + u : 256 * (s + 1) : 2], ident[:])
+            return bank
+
+        def emit(st):
+            kind, a, b = st
+            if kind == "tw":
+                T[st] = turn(w_raw[a], "wt%d" % a)
+            elif kind == "cw":
+                copy_on(
+                    CW[a],
+                    w_grp[:].bitcast(F32)[:, 512 * a : 512 * (a + 1)].rearrange("p (s r u) -> p s r u", s=2, u=2),
+                    T[("tw", a, 0)][:].rearrange("p s u r -> p s r u"),
                 )
-
-        def read_q(i):
-            q_grp[i] = keep.tile([P, P, 4], BF16, name="q_grp%d" % i, align_bytes=64)
-            nc.vector.scalar_tensor_tensor(
-                out=q_grp[i][:],
-                in0=q_bank[i][:].rearrange("p t n -> p n t"),
-                scalar=inv_sqrt_c,
-                in1=bias_s[:].unsqueeze(1).to_broadcast([P, P, 4]),
-                op0=ALU.mult,
-                op1=ALU.add,
-            )
-
-        def quant_q(i):
-            q_codes[i] = keep.tile([P, P], U32, name="q_codes%d" % i, align_bytes=64)
-            q_scales[i] = keep.tile([P, P], U8, name="q_scales%d" % i, align_bytes=64)
-            nc.vector.quantize_mx(
-                out=q_codes[i][:].bitcast(FP8X4), scales=q_scales[i][:], in_=q_grp[i][:].rearrange("p n t -> p (n t)")
-            )
-
-        sc = {}
-        mx = {}
-        ex = {}
-        ssum = {}
-        tot = {}
-
-        def scores(i):
-            sc[i] = []
-            for h in range(2):
-                s_h = psum.tile([P, C], F32, tag="bank", name="sc%d" % h)
-                nc.tensor.matmul_mx(
-                    out=s_h[:],
-                    lhsT=q_codes[i][:].bitcast(FP8X4),
-                    lhsT_scale=q_scales[i][:],
-                    rhs=k_codes[h][:].bitcast(FP8X4),
-                    rhs_scale=k_scales[h][:],
-                    start=True,
-                    stop=True,
+            elif kind == "qw":
+                nc.vector.quantize_mx(out=w_codes[:].bitcast(FP8X4), scales=w_scales[:], in_=w_grp[:])
+            elif kind == "bias":
+                nc.vector.tensor_scalar(out=bias_s[:], in0=bq_raw[:], scalar1=inv_sqrt_c, scalar2=None, op0=ALU.mult)
+            elif kind == "gx":
+                T[st] = keep.tile([P, X_CHUNKS[a], 4], BF16, name="x_grp%d" % a, align_bytes=64)
+                copy_on(GX[a], T[st][:], x_raw[a][:].rearrange("p j n -> p n j"))
+            elif kind == "qx":
+                T[("xc", a)] = keep.tile([P, X_CHUNKS[a]], U32, name="x_codes%d" % a, align_bytes=64)
+                T[("xs", a)] = keep.tile([P, X_CHUNKS[a]], U8, name="x_scales%d" % a, align_bytes=64)
+                nc.vector.quantize_mx(
+                    out=T[("xc", a)][:].bitcast(FP8X4), scales=T[("xs", a)][:], in_=T[("gx", a, 0)][:].rearrange("p n j -> p (n j)")
                 )
-                sc[i].append(s_h)
-
-        def bank_max(i, h):
-            if h == 0:
-                mx[i] = stat.tile([P, 2], F32, name="mx")
-            nc.vector.tensor_reduce(out=mx[i][:, h : h + 1], in_=sc[i][h][:], axis=AX.X, op=ALU.max)
-
-        def exponentials(i):
-            nm = stat.tile([P, 1], F32, name="nmax")
-            nc.vector.tensor_reduce(out=nm[:], in_=mx[i][:], axis=AX.X, op=ALU.max, negate=True)
-            ex[i] = soft.tile([P, NTOK], F32, name="e")
-            ssum[i] = stat.tile([P, 2], F32, name="ssum")
-            for h in range(2):
-                nc.scalar.activation(
-                    out=ex[i][:, C * h : C * (h + 1)],
-                    in_=sc[i][h][:],
-                    func=ACT.Exp,
-                    bias=nm[:],
-                    scale=1.0,
-                    accum_out=ssum[i][:, h : h + 1],
+            elif kind == "tk":
+                T[st] = turn(k_raw[a], "kt%d" % a)
+            elif kind == "ck":
+                copy_on(
+                    CK[a],
+                    k_grp[a // 2][:].bitcast(F32)[:, 512 * (a % 2) : 512 * (a % 2 + 1)].rearrange("p (r q) -> p r q", q=4),
+                    T[("tk", a, 0)][:].rearrange("p b u r -> p r (b u)"),
                 )
-
-        def row_sum(i):
-            tot[i] = stat.tile([P, 1], F32, name="tot")
-            nc.vector.tensor_reduce(out=tot[i][:], in_=ssum[i][:], axis=AX.X, op=ALU.add)
-
-        def finish(i):
-            rinv = stat.tile([P, 1], F32, name="rinv")
-            nc.vector.reciprocal(out=rinv[:], in_=tot[i][:])
-            o = soft.tile([P, NTOK], F32, name="o")
-            for h in range(2):
-                cols = slice(C * h, C * (h + 1))
-                if i >= NT - V_TAIL:
-                    nc.vector.tensor_scalar(out=o[:, cols], in0=ex[i][:, cols], scalar1=rinv[:], scalar2=None, op0=ALU.mult)
-                else:
-                    nc.gpsimd.tensor_scalar(
-                        out=o[:, cols], in0=ex[i][:, cols], scalar1=rinv[:], scalar2=0.0, op0=ALU.mult, op1=ALU.add
+            elif kind == "qk":
+                T[("kc", a)] = keep.tile([P, C], U32, name="k_codes%d" % a, align_bytes=64)
+                T[("ks", a)] = keep.tile([P, C], U8, name="k_scales%d" % a, align_bytes=64)
+                nc.vector.quantize_mx(out=T[("kc", a)][:].bitcast(FP8X4), scales=T[("ks", a)][:], in_=k_grp[a][:])
+            elif kind == "P":
+                c, j = chunk_of[a]
+                T[st] = qpp.tile([P, 4, P], BF16, tag="qp", name="qp")
+                for t in range(4):
+                    nc.tensor.matmul_mx(
+                        out=T[st][:, t, :],
+                        lhsT=w_codes[:, P * t : P * (t + 1)].bitcast(FP8X4),
+                        lhsT_scale=w_scales[:, P * t : P * (t + 1)],
+                        rhs=T[("xc", c)][:, P * j : P * (j + 1)].bitcast(FP8X4),
+                        rhs_scale=T[("xs", c)][:, P * j : P * (j + 1)],
+                        start=True,
+                        stop=True,
                     )
-                nc.sync.dma_start(out=out[0, P * i : P * (i + 1), cols], in_=o[:, cols])
+            elif kind == "R":
+                T[st] = keep.tile([P, P, 4], BF16, name="q_grp%d" % a, align_bytes=64)
+                if a in RS:
+                    for t in range(4):
+                        nc.scalar.activation(
+                            out=T[st][:, :, t],
+                            in_=T[("P", a, 0)][:, t, :],
+                            func=ACT.Identity,
+                            bias=bias_s[:, t : t + 1],
+                            scale=inv_sqrt_c,
+                        )
+                else:
+                    nc.vector.scalar_tensor_tensor(
+                        out=T[st][:],
+                        in0=T[("P", a, 0)][:].rearrange("p t n -> p n t"),
+                        scalar=inv_sqrt_c,
+                        in1=bias_s[:].unsqueeze(1).to_broadcast([P, P, 4]),
+                        op0=ALU.mult,
+                        op1=ALU.add,
+                    )
+            elif kind == "Q":
+                T[("qc", a)] = keep.tile([P, P], U32, name="q_codes%d" % a, align_bytes=64)
+                T[("qs", a)] = keep.tile([P, P], U8, name="q_scales%d" % a, align_bytes=64)
+                nc.vector.quantize_mx(
+                    out=T[("qc", a)][:].bitcast(FP8X4), scales=T[("qs", a)][:], in_=T[("R", a, 0)][:].rearrange("p n t -> p (n t)")
+                )
+            elif kind == "SC":
+                T[st] = scp.tile([P, C], F32, tag="sc", name="sc")
+                nc.tensor.matmul_mx(
+                    out=T[st][:],
+                    lhsT=T[("qc", a)][:].bitcast(FP8X4),
+                    lhsT_scale=T[("qs", a)][:],
+                    rhs=T[("kc", b)][:].bitcast(FP8X4),
+                    rhs_scale=T[("ks", b)][:],
+                    start=True,
+                    stop=True,
+                )
+            elif kind == "M":
+                if b == 0:
+                    T[("mx", a)] = keep.tile([P, 2], F32, name="mx%d" % a)
+                nc.vector.tensor_reduce(out=T[("mx", a)][:, b : b + 1], in_=T[("SC", a, b)][:], axis=AX.X, op=ALU.max)
+            elif kind == "N":
+                T[st] = keep.tile([P, 1], F32, name="nmax%d" % a)
+                nc.vector.tensor_reduce(out=T[st][:], in_=T[("mx", a)][:], axis=AX.X, op=ALU.max, negate=True)
+            elif kind == "E":
+                if b == 0:
+                    T[("e", a)] = keep.tile([P, NTOK], F32, name="e%d" % a)
+                    T[("ssum", a)] = keep.tile([P, 2], F32, name="ssum%d" % a)
+                nc.scalar.activation(
+                    out=T[("e", a)][:, C * b : C * (b + 1)],
+                    in_=T[("SC", a, b)][:],
+                    func=ACT.Exp,
+                    bias=T[("N", a, 0)][:],
+                    scale=1.0,
+                    accum_out=T[("ssum", a)][:, b : b + 1],
+                )
+            elif kind == "T":
+                T[st] = keep.tile([P, 1], F32, name="tot%d" % a)
+                nc.vector.tensor_reduce(out=T[st][:], in_=T[("ssum", a)][:], axis=AX.X, op=ALU.add)
+            elif kind == "I":
+                T[st] = keep.tile([P, 1], F32, name="rinv%d" % a)
+                nc.vector.reciprocal(out=T[st][:], in_=T[("T", a, 0)][:])
+            elif kind == "X":
+                if ("o", a) not in T:
+                    T[("o", a)] = keep.tile([P, NTOK], F32, name="o%d" % a)
+                cols = slice(C * b, C * (b + 1))
+                o = T[("o", a)]
+                e = T[("e", a)]
+                rinv = T[("I", a, 0)]
+                eng = NORM[a][b]
+                if eng == "v":
+                    nc.vector.tensor_scalar(out=o[:, cols], in0=e[:, cols], scalar1=rinv[:], scalar2=None, op0=ALU.mult)
+                elif eng == "g":
+                    nc.gpsimd.tensor_scalar(out=o[:, cols], in0=e[:, cols], scalar1=rinv[:], scalar2=0.0, op0=ALU.mult, op1=ALU.add)
+                else:
+                    nc.scalar.activation(out=o[:, cols], in_=e[:, cols], func=ACT.Copy, scale=rinv[:])
+                nc.sync.dma_start(out=out[0, P * a : P * (a + 1), cols], in_=o[:, cols])
 
-        turn_w(0)
-        turn_w(1)
-        group_x(0, "vector")
-        nc.vector.quantize_mx(out=w_codes[:].bitcast(FP8X4), scales=w_scales[:], in_=w_grp[:])
-        quant_x(0)
-        nc.vector.tensor_scalar(out=bias_s[:], in0=bq_raw[:], scalar1=inv_sqrt_c, scalar2=None, op0=ALU.mult)
-        turn_k(0)
-        turn_k(1)
-        turn_k(2)
-        group_x(1, "scalar")
-        project(0)
-        quant_k(0)
-        project(1)
-        read_q(0)
-        read_q(1)
-        quant_q(0)
-        quant_x(1)
-        turn_k(3)
-        quant_q(1)
-        project(2)
-        group_x(2, "scalar")
-        quant_k(1)
-        scores(0)
-        scores(1)
-        read_q(2)
+        def needs(st):
+            kind, a, b = st
+            if kind == "cw":
+                return [("tw", a, 0)]
+            if kind == "qw":
+                return [("cw", 0, 0), ("cw", 1, 0)]
+            if kind == "qx":
+                return [("gx", a, 0)]
+            if kind == "ck":
+                return [("tk", a, 0)]
+            if kind == "qk":
+                return [("ck", 2 * a, 0), ("ck", 2 * a + 1, 0)]
+            if kind == "P":
+                return [("qw", 0, 0), ("qx", chunk_of[a][0], 0)]
+            if kind == "R":
+                return [("P", a, 0), ("bias", 0, 0)]
+            if kind == "Q":
+                return [("R", a, 0)]
+            if kind == "SC":
+                return [("Q", a, 0), ("qk", b, 0)]
+            if kind == "M":
+                return [("SC", a, b)]
+            if kind == "N":
+                return [("M", a, 0), ("M", a, 1)]
+            if kind == "E":
+                return [("N", a, 0)]
+            if kind == "T":
+                return [("E", a, 0), ("E", a, 1)]
+            if kind == "I":
+                return [("T", a, 0)]
+            if kind == "X":
+                return [("I", a, 0)] + ([("X", a, 0)] if b == 1 else ([("X", a - 1, 1)] if a >= 1 else []))
+            return []
 
-        big = []
+        def closer(st):
+            kind, a, b = st
+            if kind == "tw":
+                return ("cw", a, 0)
+            if kind == "tk":
+                return ("ck", a, 0)
+            if kind == "SC":
+                return ("E", a, b)
+            if kind == "P":
+                return ("R", a, 0)
+            return None
+
+        pe = []
+        v = []
+        s = []
+        g = []
+        eng_of = {"g": g, "v": v, "s": s}
+        for st in PE_HEAD:
+            pe.append(st)
+        for st in V_HEAD:
+            v.append(st)
+        for st in S_HEAD:
+            s.append(st)
+
+        def norm(j):
+            for h in range(2):
+                eng_of[NORM[j][h]].append(("X", j, h))
+
         for i in range(NT):
-            big.append(("max", i, 0))
-            big.append(("max", i, 1))
-            if i + AHEAD < NT:
-                big.append(("read_q", i + AHEAD, 0))
-        pending = [(1, 1, AHEAD - 1)]
-        done = 0
-        while done < len(big) or pending:
-            if done < len(big):
-                kind, i, h = big[done]
-                if kind == "max":
-                    if h == 0 and i + AHEAD < NT:
-                        project(i + AHEAD)
-                    bank_max(i, h)
-                    if h == 1:
-                        pending.append((done + 2, 0, i))
-                else:
-                    read_q(i)
-                    pending.append((done + 2, 1, i))
-            done += 1
-            ready = sorted(p for p in pending if p[0] <= done)
-            ready = sorted(ready, key=lambda p: (p[1], p[2]))
-            pending = [p for p in pending if p[0] > done]
-            for due, rank, i in ready:
-                if rank == 0:
-                    exponentials(i)
-                    pending.append((done + 3, 2, i))
-                elif rank == 1:
-                    quant_q(i)
-                    scores(i)
-                elif rank == 2:
-                    row_sum(i)
-                    pending.append((done + 1, 3, i))
-                else:
-                    finish(i)
+            fresh = HEAD_TILES <= i + 1 < NT
+            if fresh:
+                v.append(("R", i + 1, 0))
+            if i == 1:
+                v.append(("qx", 2, 0))
+            if i >= 1:
+                v.append(("N", i - 1, 0))
+                s.append(("E", i - 1, 0))
+                s.append(("E", i - 1, 1))
+            if i >= 2:
+                v.append(("T", i - 2, 0))
+            v.append(("M", i, 0))
+            if i >= 2:
+                v.append(("I", i - 2, 0))
+                norm(i - 2)
+            if HEAD_TILES <= i + 2 < NT:
+                pe.append(("P", i + 2, 0))
+            if fresh:
+                v.append(("Q", i + 1, 0))
+                pe.append(("SC", i + 1, 0))
+                pe.append(("SC", i + 1, 1))
+            v.append(("M", i, 1))
+            if i == 0:
+                v.append(("Q", 2, 0))
+                pe.append(("SC", 2, 0))
+                pe.append(("SC", 2, 1))
+        v.append(("N", NT - 1, 0))
+        s.append(("E", NT - 1, 0))
+        s.append(("E", NT - 1, 1))
+        for j in (NT - 2, NT - 1):
+            v.append(("T", j, 0))
+            v.append(("I", j, 0))
+            norm(j)
+
+        queues = [pe, v, s, g]
+        at = [0, 0, 0, 0]
+        written = set()
+        allocs = {"sc": [], "qp": []}
+        moved = True
+        while moved:
+            moved = False
+            for q in range(4):
+                while at[q] < len(queues[q]):
+                    st = queues[q][at[q]]
+                    ok = all(n in written for n in needs(st))
+                    tag = None
+                    if st[0] in ("tw", "tk", "SC"):
+                        tag = "sc"
+                    elif st[0] == "P":
+                        tag = "qp"
+                    if ok and tag is not None:
+                        depth = SC_BUFS if tag == "sc" else QP_BUFS
+                        if len(allocs[tag]) >= depth:
+                            old = allocs[tag][len(allocs[tag]) - depth]
+                            if old is not None and old not in written:
+                                ok = False
+                    if not ok:
+                        break
+                    if tag is not None:
+                        allocs[tag].append(closer(st))
+                    emit(st)
+                    written.add(st)
+                    at[q] += 1
+                    moved = True
+        assert all(at[q] == len(queues[q]) for q in range(4)), "a queue is stuck"

@@ -306,8 +306,6 @@ def tile_visionattention_pa_kernel(tc, x, Wq, bq, k, out):
             fresh = HEAD_TILES <= i + 1 < NT
             if fresh:
                 v.append(("R", i + 1, 0))
-            if i == 1:
-                v.append(("qx", 2, 0))
             if i >= 1:
                 v.append(("N", i - 1, 0))
                 s.append(("E", i - 1, 0))
@@ -315,6 +313,8 @@ def tile_visionattention_pa_kernel(tc, x, Wq, bq, k, out):
             if i >= 2:
                 v.append(("T", i - 2, 0))
             v.append(("M", i, 0))
+            if i == 1:
+                v.append(("qx", 2, 0))
             if i >= 2:
                 v.append(("I", i - 2, 0))
                 norm(i - 2)

@@ -21,7 +21,7 @@ NT = NTOK // P
 FLOPS = 2 * NTOK * C * C + 2 * NTOK * NTOK * C
 
 X_CHUNKS = (256, 256, 512)
-LOADS = ("w0", "w1", "x0", "k0", "k1", "x1", "k2", "k3", "x2")
+LOADS = ("w0", "w1", "x0", "k0", "k1", "b0", "x1", "k2", "k3", "x2")
 SC_BUFS = 6
 QP_BUFS = 2
 GX = ("vector", "scalar", "scalar")
@@ -55,7 +55,6 @@ def tile_visionattention_pa_kernel(tc, x, Wq, bq, k, out):
         ctx.enter_context(tc.manual_schedule())
 
         bq_raw = const.tile([P, 4], BF16, name="bq_raw")
-        nc.scalar.dma_start(out=bq_raw[:], in_=bq.rearrange("(p t) -> p t", t=4))
 
         w_view = Wq.rearrange("(m t) c -> m t c", t=4)
         x_view = x[0].rearrange("(p j) h w -> p j (h w)", j=4)
@@ -65,7 +64,9 @@ def tile_visionattention_pa_kernel(tc, x, Wq, bq, k, out):
         k_raw = {}
         for name in LOADS:
             n = int(name[1:])
-            if name[0] == "w":
+            if name[0] == "b":
+                nc.sync.dma_start(out=bq_raw[:], in_=bq.rearrange("(p t) -> p t", t=4))
+            elif name[0] == "w":
                 w_raw[n] = keep.tile([P, 2, C], BF16, name="w_raw%d" % n)
                 nc.sync.dma_start(out=w_raw[n][:], in_=w_view[:, 2 * n : 2 * n + 2, :])
             elif name[0] == "x":

@@ -35,7 +35,7 @@ PE_HEAD = (
     ("tk", 2, 0), ("tk", 3, 0), ("SC", 0, 0), ("P", 2, 0), ("SC", 0, 1), ("SC", 1, 0), ("SC", 1, 1),
 )
 V_HEAD = (
-    ("gx", 0, 0), ("qw", 0, 0), ("qx", 0, 0), ("bias", 0, 0), ("ck", 1, 0), ("R", 0, 0), ("R", 1, 0), ("qk", 0, 0), ("Q", 0, 0),
+    ("gx", 0, 0), ("qw", 0, 0), ("qx", 0, 0), ("qw", 1, 0), ("bias", 0, 0), ("ck", 1, 0), ("R", 0, 0), ("R", 1, 0), ("qk", 0, 0), ("Q", 0, 0),
     ("qx", 1, 0), ("Q", 1, 0), ("qk", 1, 0), ("R", 2, 0),
 )
 S_HEAD = (
@@ -126,7 +126,10 @@ def tile_visionattention_pa_kernel(tc, x, Wq, bq, k, out):
                     T[("tw", a, 0)][:].rearrange("p s u r -> p s r u"),
                 )
             elif kind == "qw":
-                nc.vector.quantize_mx(out=w_codes[:].bitcast(FP8X4), scales=w_scales[:], in_=w_grp[:])
+                half = slice(2 * P * a, 2 * P * (a + 1))
+                nc.vector.quantize_mx(
+                    out=w_codes[:, half].bitcast(FP8X4), scales=w_scales[:, half], in_=w_grp[:, 2 * C * a : 2 * C * (a + 1)]
+                )
             elif kind == "bias":
                 nc.vector.tensor_scalar(out=bias_s[:], in0=bq_raw[:], scalar1=inv_sqrt_c, scalar2=None, op0=ALU.mult)
             elif kind == "gx":
@@ -246,7 +249,7 @@ def tile_visionattention_pa_kernel(tc, x, Wq, bq, k, out):
             if kind == "cw":
                 return [("tw", a, 0)]
             if kind == "qw":
-                return [("cw", 0, 0), ("cw", 1, 0)]
+                return [("cw", a, 0)]
             if kind == "qx":
                 return [("gx", a, 0)]
             if kind == "ck":
@@ -254,7 +257,7 @@ def tile_visionattention_pa_kernel(tc, x, Wq, bq, k, out):
             if kind == "qk":
                 return [("ck", 2 * a, 0), ("ck", 2 * a + 1, 0)]
             if kind == "P":
-                return [("qw", 0, 0), ("qx", chunk_of[a][0], 0)]
+                return [("qw", 0, 0), ("qw", 1, 0), ("qx", chunk_of[a][0], 0)]
             if kind == "R":
                 return [("P", a, 0), ("bias", 0, 0)]
             if kind == "Q":

@@ -23,16 +23,18 @@ FLOPS = 2 * NTOK * C * C + 2 * NTOK * NTOK * C
 X_CHUNKS = (256, 256, 512)
 LOADS = ("w0", "w1", "x0", "k0", "k1", "b0", "x1", "k2", "k3", "x2")
 SC_BUFS = 6
+WARM = 4
 QP_BUFS = 2
 GX = ("vector", "scalar", "scalar")
 CW = ("scalar", "scalar")
 CK = ("scalar", "vector", "scalar", "scalar")
 NORM = (("g", "g"), ("g", "g"), ("g", "g"), ("g", "g"), ("g", "g"), ("g", "g"), ("v", "v"), ("v", "v"))
-RS = ()
+SPLIT = (3,)
+READ_AFTER = {3: -1}
 HEAD_TILES = 3
 PE_HEAD = (
     ("tw", 0, 0), ("tw", 1, 0), ("tk", 0, 0), ("tk", 1, 0), ("P", 0, 0), ("P", 1, 0),
-    ("tk", 2, 0), ("tk", 3, 0), ("SC", 0, 0), ("P", 2, 0), ("SC", 0, 1), ("SC", 1, 0), ("SC", 1, 1),
+    ("tk", 2, 0), ("tk", 3, 0), ("SC", 0, 0), ("P", 2, 0), ("P", 3, 0), ("SC", 0, 1), ("SC", 1, 0), ("SC", 1, 1),
 )
 V_HEAD = (
     ("gx", 0, 0), ("qw", 0, 0), ("qx", 0, 0), ("qw", 1, 0), ("bias", 0, 0), ("ck", 1, 0), ("R", 0, 0), ("R", 1, 0), ("qk", 0, 0), ("Q", 0, 0),
@@ -81,6 +83,12 @@ def tile_visionattention_pa_kernel(tc, x, Wq, bq, k, out):
         make_identity(nc, ident[:])
         warm_in = const.tile([P, 1], F32, name="warm_in")
         warm_out = const.tile([P, 1], F32, name="warm_out")
+        pe_words = const.tile([P, C // 2], F32, name="pe_words")
+        nc.vector.memset(pe_words[:], 0.0)
+        pe_zeros = pe_words[:].bitcast(BF16)
+        pe_bank = scp.tile([P, C], F32, tag="sc", name="pe_bank")
+        for r in range(WARM):
+            nc.tensor.matmul(out=pe_bank[:], lhsT=pe_zeros[:, 0:P], rhs=pe_zeros, start=True, stop=True)
         nc.vector.memset(warm_in[:], 0.0)
         nc.scalar.activation(out=warm_out[:], in_=warm_in[:], func=ACT.Exp)
         bias_s = const.tile([P, 4], F32, name="bias_s")
@@ -167,30 +175,35 @@ def tile_visionattention_pa_kernel(tc, x, Wq, bq, k, out):
                         stop=True,
                     )
             elif kind == "R":
-                T[st] = keep.tile([P, P, 4], BF16, name="q_grp%d" % a, align_bytes=64)
-                if a in RS:
-                    for t in range(4):
-                        nc.scalar.activation(
-                            out=T[st][:, :, t],
-                            in_=T[("P", a, 0)][:, t, :],
-                            func=ACT.Identity,
-                            bias=bias_s[:, t : t + 1],
-                            scale=inv_sqrt_c,
-                        )
-                else:
-                    nc.vector.scalar_tensor_tensor(
-                        out=T[st][:],
-                        in0=T[("P", a, 0)][:].rearrange("p t n -> p n t"),
-                        scalar=inv_sqrt_c,
-                        in1=bias_s[:].unsqueeze(1).to_broadcast([P, P, 4]),
-                        op0=ALU.mult,
-                        op1=ALU.add,
-                    )
+                T[("qg", a)] = keep.tile([P, P, 4], BF16, name="q_grp%d" % a, align_bytes=64)
+                nc.vector.scalar_tensor_tensor(
+                    out=T[("qg", a)][:],
+                    in0=T[("P", a, 0)][:].rearrange("p t n -> p n t"),
+                    scalar=inv_sqrt_c,
+                    in1=bias_s[:].unsqueeze(1).to_broadcast([P, P, 4]),
+                    op0=ALU.mult,
+                    op1=ALU.add,
+                )
+            elif kind == "RS":
+                T[st] = keep.tile([P, P, 4], F32, name="q_mid%d" % a)
+                nc.scalar.activation(
+                    out=T[st][:], in_=T[("P", a, 0)][:].rearrange("p t n -> p n t"), func=ACT.Copy, scale=inv_sqrt_c
+                )
+            elif kind == "RG":
+                if b == 0:
+                    T[("qg", a)] = keep.tile([P, P, 4], BF16, name="q_grp%d" % a, align_bytes=64)
+                toks = slice(64 * b, 64 * (b + 1))
+                nc.gpsimd.tensor_tensor(
+                    out=T[("qg", a)][:, toks, :],
+                    in0=T[("RS", a, 0)][:, toks, :],
+                    in1=bias_s[:].unsqueeze(1).to_broadcast([P, 64, 4]),
+                    op=ALU.add,
+                )
             elif kind == "Q":
                 T[("qc", a)] = keep.tile([P, P], U32, name="q_codes%d" % a, align_bytes=64)
                 T[("qs", a)] = keep.tile([P, P], U8, name="q_scales%d" % a, align_bytes=64)
                 nc.vector.quantize_mx(
-                    out=T[("qc", a)][:].bitcast(FP8X4), scales=T[("qs", a)][:], in_=T[("R", a, 0)][:].rearrange("p n t -> p (n t)")
+                    out=T[("qc", a)][:].bitcast(FP8X4), scales=T[("qs", a)][:], in_=T[("qg", a)][:].rearrange("p n t -> p (n t)")
                 )
             elif kind == "SC":
                 T[st] = scp.tile([P, C], F32, tag="sc", name="sc")
@@ -260,8 +273,12 @@ def tile_visionattention_pa_kernel(tc, x, Wq, bq, k, out):
                 return [("qw", 0, 0), ("qw", 1, 0), ("qx", chunk_of[a][0], 0)]
             if kind == "R":
                 return [("P", a, 0), ("bias", 0, 0)]
+            if kind == "RS":
+                return [("P", a, 0)]
+            if kind == "RG":
+                return [("RS", a, 0), ("bias", 0, 0)]
             if kind == "Q":
-                return [("R", a, 0)]
+                return [("RG", a, 0), ("RG", a, 1)] if a in SPLIT else [("R", a, 0)]
             if kind == "SC":
                 return [("Q", a, 0), ("qk", b, 0)]
             if kind == "M":
@@ -287,7 +304,7 @@ def tile_visionattention_pa_kernel(tc, x, Wq, bq, k, out):
             if kind == "SC":
                 return ("E", a, b)
             if kind == "P":
-                return ("R", a, 0)
+                return ("RS", a, 0) if a in SPLIT else ("R", a, 0)
             return None
 
         pe = []
@@ -306,26 +323,49 @@ def tile_visionattention_pa_kernel(tc, x, Wq, bq, k, out):
             for h in range(2):
                 eng_of[NORM[j][h]].append(("X", j, h))
 
+        def read_ahead(i):
+            for j in SPLIT:
+                if READ_AFTER[j] == i:
+                    if i >= 0:
+                        pe.append(("P", j, 0))
+                    s.append(("RS", j, 0))
+                    for h in range(2):
+                        g.append(("RG", j, h))
+
+        read_ahead(-1)
+
         for i in range(NT):
             fresh = HEAD_TILES <= i + 1 < NT
-            if fresh:
+            split = i + 1 in SPLIT
+            if split:
+                v.append(("M", i, 0))
+            elif fresh:
                 v.append(("R", i + 1, 0))
             if i >= 1:
                 v.append(("N", i - 1, 0))
                 s.append(("E", i - 1, 0))
                 s.append(("E", i - 1, 1))
-            if i >= 2:
+                read_ahead(i - 1)
+            if i >= 2 and i not in SPLIT:
                 v.append(("T", i - 2, 0))
-            v.append(("M", i, 0))
             if i == 1:
                 v.append(("qx", 2, 0))
+            if not split and ("M", i, 0) not in V_HEAD:
+                v.append(("M", i, 0))
+            if split:
+                v.append(("Q", i + 1, 0))
+            if i in SPLIT:
+                v.append(("T", i - 2, 0))
+                if fresh and not split:
+                    v.append(("Q", i + 1, 0))
             if i >= 2:
                 v.append(("I", i - 2, 0))
                 norm(i - 2)
-            if HEAD_TILES <= i + 2 < NT:
+            if HEAD_TILES <= i + 2 < NT and i + 2 not in SPLIT:
                 pe.append(("P", i + 2, 0))
-            if fresh:
+            if fresh and not split and i not in SPLIT:
                 v.append(("Q", i + 1, 0))
+            if fresh:
                 pe.append(("SC", i + 1, 0))
                 pe.append(("SC", i + 1, 1))
             v.append(("M", i, 1))
@@ -343,8 +383,8 @@ def tile_visionattention_pa_kernel(tc, x, Wq, bq, k, out):
 
         queues = [pe, v, s, g]
         at = [0, 0, 0, 0]
-        written = set()
-        allocs = {"sc": [], "qp": []}
+        written = {("warm", 0, 0)}
+        allocs = {"sc": [("warm", 0, 0)], "qp": []}
         moved = True
         while moved:
             moved = False

@@ -23,12 +23,13 @@ FLOPS = 2 * NTOK * C * C + 2 * NTOK * NTOK * C
 X_CHUNKS = (256, 256, 512)
 LOADS = ("w0", "w1", "x0", "k0", "k1", "b0", "x1", "k2", "k3", "x2")
 SC_BUFS = 6
-WARM = 4
+WARM = 3
 QP_BUFS = 2
 GX = ("vector", "scalar", "scalar")
 CW = ("scalar", "scalar")
 CK = ("scalar", "vector", "scalar", "scalar")
 NORM = (("g", "g"), ("g", "g"), ("g", "g"), ("g", "g"), ("g", "g"), ("g", "g"), ("v", "v"), ("v", "v"))
+ONE_STORE = (0, 1, 2, 3)
 SPLIT = (3,)
 READ_AFTER = {3: -1}
 HEAD_TILES = 3
@@ -255,7 +256,10 @@ def tile_visionattention_pa_kernel(tc, x, Wq, bq, k, out):
                     nc.gpsimd.tensor_scalar(out=o[:, cols], in0=e[:, cols], scalar1=rinv[:], scalar2=0.0, op0=ALU.mult, op1=ALU.add)
                 else:
                     nc.scalar.activation(out=o[:, cols], in_=e[:, cols], func=ACT.Copy, scale=rinv[:])
-                nc.sync.dma_start(out=out[0, P * a : P * (a + 1), cols], in_=o[:, cols])
+                if a not in ONE_STORE:
+                    nc.sync.dma_start(out=out[0, P * a : P * (a + 1), cols], in_=o[:, cols])
+                elif b == 1:
+                    nc.sync.dma_start(out=out[0, P * a : P * (a + 1), :], in_=o[:])
 
         def needs(st):
             kind, a, b = st

from contextlib import ExitStack
import math

import concourse.mybir as mybir
from concourse.masks import make_identity

F32 = mybir.dt.float32
BF16 = mybir.dt.bfloat16
U32 = mybir.dt.uint32
U8 = mybir.dt.uint8
FP8X4 = mybir.dt.float8_e4m3fn_x4
ALU = mybir.AluOpType
ACT = mybir.ActivationFunctionType
AX = mybir.AxisListType

P = 128
C = 512
NTOK = 1024
NT = NTOK // P

FLOPS = 2 * NTOK * C * C + 2 * NTOK * NTOK * C

X_CHUNKS = (256, 256, 512)
LOADS = ("w0", "w1", "x0", "k0", "k1", "b0", "x1", "k2", "k3", "x2")
SC_BUFS = 6
WARM = 3
QP_BUFS = 2
GX = ("vector", "scalar", "scalar")
CW = ("scalar", "scalar")
CK = ("scalar", "vector", "scalar", "scalar")
NORM = (("g", "g"), ("g", "g"), ("g", "g"), ("g", "g"), ("g", "g"), ("g", "g"), ("v", "v"), ("v", "v"))
ONE_STORE = (0, 1, 2, 3)
SPLIT = (3,)
READ_AFTER = {3: -1}
HEAD_TILES = 3
PE_HEAD = (
    ("tw", 0, 0), ("tw", 1, 0), ("tk", 0, 0), ("tk", 1, 0), ("P", 0, 0), ("P", 1, 0),
    ("tk", 2, 0), ("tk", 3, 0), ("SC", 0, 0), ("P", 2, 0), ("P", 3, 0), ("SC", 0, 1), ("SC", 1, 0), ("SC", 1, 1),
)
V_HEAD = (
    ("gx", 0, 0), ("qw", 0, 0), ("qx", 0, 0), ("qw", 1, 0), ("bias", 0, 0), ("ck", 1, 0), ("R", 0, 0), ("R", 1, 0), ("qk", 0, 0), ("Q", 0, 0),
    ("qx", 1, 0), ("Q", 1, 0), ("qk", 1, 0), ("R", 2, 0),
)
S_HEAD = (
    ("cw", 0, 0), ("cw", 1, 0), ("ck", 0, 0), ("gx", 1, 0), ("ck", 2, 0), ("ck", 3, 0), ("gx", 2, 0),
)


def tile_visionattention_pa_kernel(tc, x, Wq, bq, k, out):
    nc = tc.nc
    inv_sqrt_c = 1.0 / math.sqrt(C)

    with ExitStack() as ctx:
        const = ctx.enter_context(tc.tile_pool(name="const", bufs=1))
        keep = ctx.enter_context(tc.tile_pool(name="keep", bufs=1))
        scp = ctx.enter_context(tc.psum_pool(name="scp", bufs=SC_BUFS))
        qpp = ctx.enter_context(tc.psum_pool(name="qpp", bufs=QP_BUFS))
        ctx.enter_context(tc.manual_schedule())

        bq_raw = const.tile([P, 4], BF16, name="bq_raw")

        w_view = Wq.rearrange("(m t) c -> m t c", t=4)
        x_view = x[0].rearrange("(p j) h w -> p j (h w)", j=4)
        k_view = k[0].rearrange("(g r b) c -> r g b c", r=P, b=2)
        w_raw = {}
        x_raw = {}
        k_raw = {}
        for name in LOADS:
            n = int(name[1:])
            if name[0] == "b":
                nc.sync.dma_start(out=bq_raw[:], in_=bq.rearrange("(p t) -> p t", t=4))
            elif name[0] == "w":
                w_raw[n] = keep.tile([P, 2, C], BF16, name="w_raw%d" % n)
                nc.sync.dma_start(out=w_raw[n][:], in_=w_view[:, 2 * n : 2 * n + 2, :])
            elif name[0] == "x":
                n0 = sum(X_CHUNKS[:n])
                x_raw[n] = keep.tile([P, 4, X_CHUNKS[n]], BF16, name="x_raw%d" % n)
                nc.sync.dma_start(out=x_raw[n][:], in_=x_view[:, :, n0 : n0 + X_CHUNKS[n]])
            else:
                k_raw[n] = keep.tile([P, 2, C], BF16, name="k_raw%d" % n)
                nc.sync.dma_start(out=k_raw[n][:], in_=k_view[:, n, :, :])

        ident = const.tile([P, P], F32, name="ident")
        make_identity(nc, ident[:])
        warm_in = const.tile([P, 1], F32, name="warm_in")
        warm_out = const.tile([P, 1], F32, name="warm_out")
        pe_words = const.tile([P, C // 2], F32, name="pe_words")
        nc.vector.memset(pe_words[:], 0.0)
        pe_zeros = pe_words[:].bitcast(BF16)
        pe_bank = scp.tile([P, C], F32, tag="sc", name="pe_bank")
        for r in range(WARM):
            nc.tensor.matmul(out=pe_bank[:], lhsT=pe_zeros[:, 0:P], rhs=pe_zeros, start=True, stop=True)
        nc.vector.memset(warm_in[:], 0.0)
        nc.scalar.activation(out=warm_out[:], in_=warm_in[:], func=ACT.Exp)
        bias_s = const.tile([P, 4], F32, name="bias_s")

        w_grp = keep.tile([P, 4 * C], BF16, name="w_grp", align_bytes=64)
        w_codes = keep.tile([P, C], U32, name="w_codes", align_bytes=64)
        w_scales = keep.tile([P, C], U8, name="w_scales", align_bytes=64)
        k_grp = {}
        for h in range(2):
            k_grp[h] = keep.tile([P, 4 * C], BF16, name="k_grp%d" % h, align_bytes=64)

        T = {}

        chunk_of = []
        for c in range(len(X_CHUNKS)):
            for j in range(X_CHUNKS[c] // P):
                chunk_of.append((c, j))

        def copy_on(engine, dst, src):
            if engine == "scalar":
                nc.scalar.copy(out=dst, in_=src)
            elif engine == "vector":
                nc.vector.tensor_copy(out=dst, in_=src)
            else:
                nc.gpsimd.tensor_scalar(out=dst, in0=src, scalar1=1.0, scalar2=0.0, op0=ALU.mult, op1=ALU.add)

        def turn(raw, name):
            words = raw[:].rearrange("r s c -> r (s c)").bitcast(F32)
            bank = scp.tile([P, 2, 2, P], F32, tag="sc", name=name)
            for s in range(2):
                for u in range(2):
                    nc.tensor.transpose(bank[:, s, u, :], words[:, 256 * s + u : 256 * (s + 1) : 2], ident[:])
            return bank

        def emit(st):
            kind, a, b = st
            if kind == "tw":
                T[st] = turn(w_raw[a], "wt%d" % a)
            elif kind == "cw":
                copy_on(
                    CW[a],
                    w_grp[:].bitcast(F32)[:, 512 * a : 512 * (a + 1)].rearrange("p (s r u) -> p s r u", s=2, u=2),
                    T[("tw", a, 0)][:].rearrange("p s u r -> p s r u"),
                )
            elif kind == "qw":
                half = slice(2 * P * a, 2 * P * (a + 1))
                nc.vector.quantize_mx(
                    out=w_codes[:, half].bitcast(FP8X4), scales=w_scales[:, half], in_=w_grp[:, 2 * C * a : 2 * C * (a + 1)]
                )
            elif kind == "bias":
                nc.vector.tensor_scalar(out=bias_s[:], in0=bq_raw[:], scalar1=inv_sqrt_c, scalar2=None, op0=ALU.mult)
            elif kind == "gx":
                T[st] = keep.tile([P, X_CHUNKS[a], 4], BF16, name="x_grp%d" % a, align_bytes=64)
                copy_on(GX[a], T[st][:], x_raw[a][:].rearrange("p j n -> p n j"))
            elif kind == "qx":
                T[("xc", a)] = keep.tile([P, X_CHUNKS[a]], U32, name="x_codes%d" % a, align_bytes=64)
                T[("xs", a)] = keep.tile([P, X_CHUNKS[a]], U8, name="x_scales%d" % a, align_bytes=64)
                nc.vector.quantize_mx(
                    out=T[("xc", a)][:].bitcast(FP8X4), scales=T[("xs", a)][:], in_=T[("gx", a, 0)][:].rearrange("p n j -> p (n j)")
                )
            elif kind == "tk":
                T[st] = turn(k_raw[a], "kt%d" % a)
            elif kind == "ck":
                copy_on(
                    CK[a],
                    k_grp[a // 2][:].bitcast(F32)[:, 512 * (a % 2) : 512 * (a % 2 + 1)].rearrange("p (r q) -> p r q", q=4),
                    T[("tk", a, 0)][:].rearrange("p b u r -> p r (b u)"),
                )
            elif kind == "qk":
                T[("kc", a)] = keep.tile([P, C], U32, name="k_codes%d" % a, align_bytes=64)
                T[("ks", a)] = keep.tile([P, C], U8, name="k_scales%d" % a, align_bytes=64)
                nc.vector.quantize_mx(out=T[("kc", a)][:].bitcast(FP8X4), scales=T[("ks", a)][:], in_=k_grp[a][:])
            elif kind == "P":
                c, j = chunk_of[a]
                T[st] = qpp.tile([P, 4, P], BF16, tag="qp", name="qp")
                for t in range(4):
                    nc.tensor.matmul_mx(
                        out=T[st][:, t, :],
                        lhsT=w_codes[:, P * t : P * (t + 1)].bitcast(FP8X4),
                        lhsT_scale=w_scales[:, P * t : P * (t + 1)],
                        rhs=T[("xc", c)][:, P * j : P * (j + 1)].bitcast(FP8X4),
                        rhs_scale=T[("xs", c)][:, P * j : P * (j + 1)],
                        start=True,
                        stop=True,
                    )
            elif kind == "R":
                T[("qg", a)] = keep.tile([P, P, 4], BF16, name="q_grp%d" % a, align_bytes=64)
                nc.vector.scalar_tensor_tensor(
                    out=T[("qg", a)][:],
                    in0=T[("P", a, 0)][:].rearrange("p t n -> p n t"),
                    scalar=inv_sqrt_c,
                    in1=bias_s[:].unsqueeze(1).to_broadcast([P, P, 4]),
                    op0=ALU.mult,
                    op1=ALU.add,
                )
            elif kind == "RS":
                T[st] = keep.tile([P, P, 4], F32, name="q_mid%d" % a)
                nc.scalar.activation(
                    out=T[st][:], in_=T[("P", a, 0)][:].rearrange("p t n -> p n t"), func=ACT.Copy, scale=inv_sqrt_c
                )
            elif kind == "RG":
                if b == 0:
                    T[("qg", a)] = keep.tile([P, P, 4], BF16, name="q_grp%d" % a, align_bytes=64)
                toks = slice(64 * b, 64 * (b + 1))
                nc.gpsimd.tensor_tensor(
                    out=T[("qg", a)][:, toks, :],
                    in0=T[("RS", a, 0)][:, toks, :],
                    in1=bias_s[:].unsqueeze(1).to_broadcast([P, 64, 4]),
                    op=ALU.add,
                )
            elif kind == "Q":
                T[("qc", a)] = keep.tile([P, P], U32, name="q_codes%d" % a, align_bytes=64)
                T[("qs", a)] = keep.tile([P, P], U8, name="q_scales%d" % a, align_bytes=64)
                nc.vector.quantize_mx(
                    out=T[("qc", a)][:].bitcast(FP8X4), scales=T[("qs", a)][:], in_=T[("qg", a)][:].rearrange("p n t -> p (n t)")
                )
            elif kind == "SC":
                T[st] = scp.tile([P, C], F32, tag="sc", name="sc")
                nc.tensor.matmul_mx(
                    out=T[st][:],
                    lhsT=T[("qc", a)][:].bitcast(FP8X4),
                    lhsT_scale=T[("qs", a)][:],
                    rhs=T[("kc", b)][:].bitcast(FP8X4),
                    rhs_scale=T[("ks", b)][:],
                    start=True,
                    stop=True,
                )
            elif kind == "M":
                if b == 0:
                    T[("mx", a)] = keep.tile([P, 2], F32, name="mx%d" % a)
                nc.vector.tensor_reduce(out=T[("mx", a)][:, b : b + 1], in_=T[("SC", a, b)][:], axis=AX.X, op=ALU.max)
            elif kind == "N":
                T[st] = keep.tile([P, 1], F32, name="nmax%d" % a)
                nc.vector.tensor_reduce(out=T[st][:], in_=T[("mx", a)][:], axis=AX.X, op=ALU.max, negate=True)
            elif kind == "E":
                if b == 0:
                    T[("e", a)] = keep.tile([P, NTOK], F32, name="e%d" % a)
                    T[("ssum", a)] = keep.tile([P, 2], F32, name="ssum%d" % a)
                nc.scalar.activation(
                    out=T[("e", a)][:, C * b : C * (b + 1)],
                    in_=T[("SC", a, b)][:],
                    func=ACT.Exp,
                    bias=T[("N", a, 0)][:],
                    scale=1.0,
                    accum_out=T[("ssum", a)][:, b : b + 1],
                )
            elif kind == "T":
                T[st] = keep.tile([P, 1], F32, name="tot%d" % a)
                nc.vector.tensor_reduce(out=T[st][:], in_=T[("ssum", a)][:], axis=AX.X, op=ALU.add)
            elif kind == "I":
                T[st] = keep.tile([P, 1], F32, name="rinv%d" % a)
                nc.vector.reciprocal(out=T[st][:], in_=T[("T", a, 0)][:])
            elif kind == "X":
                if ("o", a) not in T:
                    T[("o", a)] = keep.tile([P, NTOK], F32, name="o%d" % a)
                cols = slice(C * b, C * (b + 1))
                o = T[("o", a)]
                e = T[("e", a)]
                rinv = T[("I", a, 0)]
                eng = NORM[a][b]
                if eng == "v":
                    nc.vector.tensor_scalar(out=o[:, cols], in0=e[:, cols], scalar1=rinv[:], scalar2=None, op0=ALU.mult)
                elif eng == "g":
                    nc.gpsimd.tensor_scalar(out=o[:, cols], in0=e[:, cols], scalar1=rinv[:], scalar2=0.0, op0=ALU.mult, op1=ALU.add)
                else:
                    nc.scalar.activation(out=o[:, cols], in_=e[:, cols], func=ACT.Copy, scale=rinv[:])
                if a not in ONE_STORE:
                    nc.sync.dma_start(out=out[0, P * a : P * (a + 1), cols], in_=o[:, cols])
                elif b == 1:
                    nc.sync.dma_start(out=out[0, P * a : P * (a + 1), :], in_=o[:])

        def needs(st):
            kind, a, b = st
            if kind == "cw":
                return [("tw", a, 0)]
            if kind == "qw":
                return [("cw", a, 0)]
            if kind == "qx":
                return [("gx", a, 0)]
            if kind == "ck":
                return [("tk", a, 0)]
            if kind == "qk":
                return [("ck", 2 * a, 0), ("ck", 2 * a + 1, 0)]
            if kind == "P":
                return [("qw", 0, 0), ("qw", 1, 0), ("qx", chunk_of[a][0], 0)]
            if kind == "R":
                return [("P", a, 0), ("bias", 0, 0)]
            if kind == "RS":
                return [("P", a, 0)]
            if kind == "RG":
                return [("RS", a, 0), ("bias", 0, 0)]
            if kind == "Q":
                return [("RG", a, 0), ("RG", a, 1)] if a in SPLIT else [("R", a, 0)]
            if kind == "SC":
                return [("Q", a, 0), ("qk", b, 0)]
            if kind == "M":
                return [("SC", a, b)]
            if kind == "N":
                return [("M", a, 0), ("M", a, 1)]
            if kind == "E":
                return [("N", a, 0)]
            if kind == "T":
                return [("E", a, 0), ("E", a, 1)]
            if kind == "I":
                return [("T", a, 0)]
            if kind == "X":
                return [("I", a, 0)] + ([("X", a, 0)] if b == 1 else ([("X", a - 1, 1)] if a >= 1 else []))
            return []

        def closer(st):
            kind, a, b = st
            if kind == "tw":
                return ("cw", a, 0)
            if kind == "tk":
                return ("ck", a, 0)
            if kind == "SC":
                return ("E", a, b)
            if kind == "P":
                return ("RS", a, 0) if a in SPLIT else ("R", a, 0)
            return None

        pe = []
        v = []
        s = []
        g = []
        eng_of = {"g": g, "v": v, "s": s}
        for st in PE_HEAD:
            pe.append(st)
        for st in V_HEAD:
            v.append(st)
        for st in S_HEAD:
            s.append(st)

        def norm(j):
            for h in range(2):
                eng_of[NORM[j][h]].append(("X", j, h))

        def read_ahead(i):
            for j in SPLIT:
                if READ_AFTER[j] == i:
                    if i >= 0:
                        pe.append(("P", j, 0))
                    s.append(("RS", j, 0))
                    for h in range(2):
                        g.append(("RG", j, h))

        read_ahead(-1)

        for i in range(NT):
            fresh = HEAD_TILES <= i + 1 < NT
            split = i + 1 in SPLIT
            if split:
                v.append(("M", i, 0))
            elif fresh:
                v.append(("R", i + 1, 0))
            if i >= 1:
                v.append(("N", i - 1, 0))
                s.append(("E", i - 1, 0))
                s.append(("E", i - 1, 1))
                read_ahead(i - 1)
            if i >= 2 and i not in SPLIT:
                v.append(("T", i - 2, 0))
            if i == 1:
                v.append(("qx", 2, 0))
            if not split and ("M", i, 0) not in V_HEAD:
                v.append(("M", i, 0))
            if split:
                v.append(("Q", i + 1, 0))
            if i in SPLIT:
                v.append(("T", i - 2, 0))
                if fresh and not split:
                    v.append(("Q", i + 1, 0))
            if i >= 2:
                v.append(("I", i - 2, 0))
                norm(i - 2)
            if HEAD_TILES <= i + 2 < NT and i + 2 not in SPLIT:
                pe.append(("P", i + 2, 0))
            if fresh and not split and i not in SPLIT:
                v.append(("Q", i + 1, 0))
            if fresh:
                pe.append(("SC", i + 1, 0))
                pe.append(("SC", i + 1, 1))
            v.append(("M", i, 1))
            if i == 0:
                v.append(("Q", 2, 0))
                pe.append(("SC", 2, 0))
                pe.append(("SC", 2, 1))
        v.append(("N", NT - 1, 0))
        s.append(("E", NT - 1, 0))
        s.append(("E", NT - 1, 1))
        for j in (NT - 2, NT - 1):
            v.append(("T", j, 0))
            v.append(("I", j, 0))
            norm(j)

        queues = [pe, v, s, g]
        at = [0, 0, 0, 0]
        written = {("warm", 0, 0)}
        allocs = {"sc": [("warm", 0, 0)], "qp": []}
        moved = True
        while moved:
            moved = False
            for q in range(4):
                while at[q] < len(queues[q]):
                    st = queues[q][at[q]]
                    ok = all(n in written for n in needs(st))
                    tag = None
                    if st[0] in ("tw", "tk", "SC"):
                        tag = "sc"
                    elif st[0] == "P":
                        tag = "qp"
                    if ok and tag is not None:
                        depth = SC_BUFS if tag == "sc" else QP_BUFS
                        if len(allocs[tag]) >= depth:
                            old = allocs[tag][len(allocs[tag]) - depth]
                            if old is not None and old not in written:
                                ok = False
                    if not ok:
                        break
                    if tag is not None:
                        allocs[tag].append(closer(st))
                    emit(st)
                    written.add(st)
                    at[q] += 1
                    moved = True
        assert all(at[q] == len(queues[q]) for q in range(4)), "a queue is stuck"
